import numpy as np
import ml_dtypes


def mxq(x, axis, fmt="e4m3"):
    dtype, down = {"e4m3": (ml_dtypes.float8_e4m3fn, 7), "e5m2": (ml_dtypes.float8_e5m2, 14)}[fmt]
    v = np.moveaxis(np.asarray(x, np.float32).astype(ml_dtypes.bfloat16).astype(np.float64), axis, -1)
    blocks = v.reshape(v.shape[:-1] + (-1, 32))
    amax = np.abs(blocks).max(-1, keepdims=True)
    byte = np.maximum(np.where(amax > 0, np.frexp(amax)[1] - 1 + 127, 0) - down, 1)
    scale = np.exp2(byte - 127.0)
    codes = (blocks / scale).astype(np.float32).astype(dtype).astype(np.float64)
    return np.moveaxis((codes * scale).reshape(v.shape), -1, axis)


WIDE = False


def mx_kscale(k):
    if not WIDE:
        return np.ones(k)
    levels = np.array([10, -10, 5, -5, 0])
    a = np.random.permutation(np.resize(levels, k // 512 * 4)).reshape(k // 512, 4)
    idx = np.arange(k)
    return np.exp2(a[idx // 512, idx % 128 // 32])


BF16 = ml_dtypes.bfloat16


def bf(x):
    return np.asarray(x, np.float32).astype(BF16)


def f64(x):
    return np.asarray(x).astype(np.float64)


E2M1 = np.array([0.0, 0.5, 1.0, 1.5, 2.0, 3.0, 4.0, 6.0, -0.0, -0.5, -1.0, -1.5, -2.0, -3.0, -4.0, -6.0])


def pack_weight(w, fmt):
    k, n = w.shape
    w = f64(bf(w)).reshape(k // 32, 32, n)
    amax = np.abs(w).max(1)
    if fmt == "e4m3":
        byte = np.frexp(amax)[1] - 1 + 127 - 7
    else:
        mant, ex = np.frexp(amax / 6.0)
        byte = np.where(mant > 0.5, ex, ex - 1) + 127
    byte = np.clip(np.where(amax > 0, byte, 1), 1, 254)
    scaled = (w * np.exp2(127.0 - byte)[:, None, :]).reshape(k, n).astype(np.float32)
    by_word = np.ascontiguousarray(scaled.reshape(k // 512, 128, 4, n).transpose(0, 1, 3, 2))
    if fmt == "e4m3":
        words = by_word.astype(ml_dtypes.float8_e4m3fn).view(np.uint8)
    else:
        c = by_word.astype(ml_dtypes.float4_e2m1fn).view(np.uint8) & 0xF
        words = c[..., 0::2] | (c[..., 1::2] << 4)
    return np.ascontiguousarray(words), np.ascontiguousarray(byte.astype(np.uint8).reshape(k // 512, 16, n))


def unpack_weight(words, scales, fmt):
    g, p, n, _ = words.shape
    if fmt == "e4m3":
        vals = np.ascontiguousarray(words).view(ml_dtypes.float8_e4m3fn).astype(np.float64)
    else:
        nib = np.empty((g, p, n, 4), np.uint8)
        nib[..., 0::2] = words & 0xF
        nib[..., 1::2] = words >> 4
        vals = E2M1[nib]
    vals = vals * np.repeat(np.exp2(scales.astype(np.float64) - 127.0), 8, axis=1)[..., None]
    return vals.transpose(0, 1, 3, 2).reshape(g * 512, n)


B, I, H = 128, 1024, 1024
K = H + I
FMT = "e4m3"
NAMES = ["w_f_light", "w_i_light", "w_c_light", "w_o_light",
         "w_f_light_temp", "w_i_light_temp", "w_c_light_temp", "w_o_light_temp"]


def sigmoid(v):
    return 1.0 / (1.0 + np.exp(-v))


def setup_inputs():
    s = mx_kscale(K)
    inp = {
        "y": bf(np.random.standard_normal((B, I)) * s[H:]),
        "h_light": bf(np.random.standard_normal((B, H)) * s[:H]),
        "c_light": bf(np.random.standard_normal((B, H))),
        "h_temp": bf(np.random.standard_normal((B, H)) * s[:H]),
        "c_temp": bf(np.random.standard_normal((B, H))),
    }
    for n in NAMES:
        w = np.random.standard_normal((H, K)) / np.sqrt(K) / s
        words, scales = pack_weight(np.ascontiguousarray(w.T), FMT)
        inp[n + "_words"] = words
        inp[n + "_scales"] = scales
        inp["b" + n[1:]] = bf(np.random.standard_normal(H) * 0.5)
    return inp


def _branch(hx, wf, b_f, wi, b_i, wc, b_c, wo, b_o):
    W = np.concatenate([wf, wi, wc, wo], axis=1)
    b = np.concatenate([b_f, b_i, b_c, b_o], axis=0)
    z = (mxq(hx, 1, "e4m3") @ W) + b
    zf, zi, zc, zo = np.split(z, 4, axis=1)
    return sigmoid(zf), sigmoid(zi), np.tanh(zc), sigmoid(zo)


def reference(y, h_light, c_light, h_temp, c_temp,
              w_f_light_words, w_f_light_scales, b_f_light, w_i_light_words, w_i_light_scales, b_i_light,
              w_c_light_words, w_c_light_scales, b_c_light, w_o_light_words, w_o_light_scales, b_o_light,
              w_f_light_temp_words, w_f_light_temp_scales, b_f_light_temp,
              w_i_light_temp_words, w_i_light_temp_scales, b_i_light_temp,
              w_c_light_temp_words, w_c_light_temp_scales, b_c_light_temp,
              w_o_light_temp_words, w_o_light_temp_scales, b_o_light_temp):
    y, h_light, c_light, h_temp = f64(y), f64(h_light), f64(c_light), f64(h_temp)
    hx_l = np.concatenate([h_light, y], axis=1)
    hx_t = np.concatenate([h_temp, y], axis=1)
    f1, i1, ch1, o1 = _branch(hx_l, unpack_weight(w_f_light_words, w_f_light_scales, FMT), f64(b_f_light),
                              unpack_weight(w_i_light_words, w_i_light_scales, FMT), f64(b_i_light),
                              unpack_weight(w_c_light_words, w_c_light_scales, FMT), f64(b_c_light),
                              unpack_weight(w_o_light_words, w_o_light_scales, FMT), f64(b_o_light))
    f2, i2, ch2, o2 = _branch(hx_t, unpack_weight(w_f_light_temp_words, w_f_light_temp_scales, FMT), f64(b_f_light_temp),
                              unpack_weight(w_i_light_temp_words, w_i_light_temp_scales, FMT), f64(b_i_light_temp),
                              unpack_weight(w_c_light_temp_words, w_c_light_temp_scales, FMT), f64(b_c_light_temp),
                              unpack_weight(w_o_light_temp_words, w_o_light_temp_scales, FMT), f64(b_o_light_temp))
    c_new = (f1 * c_light + i1 * ch1) + (f2 * c_light + i2 * ch2)
    h_new = (o1 + o2) * np.tanh(c_new)
    return h_new, c_new

@@ -1,0 +1,218 @@
+from contextlib import ExitStack
+
+import concourse.mybir as mybir
+from concourse.masks import make_identity
+
+F32 = mybir.dt.float32
+BF16 = mybir.dt.bfloat16
+I32 = mybir.dt.int32
+U32 = mybir.dt.uint32
+U8 = mybir.dt.uint8
+FP8X4 = mybir.dt.float8_e4m3fn_x4
+ALU = mybir.AluOpType
+ACT = mybir.ActivationFunctionType
+
+P = 128
+H = 1024
+BANK = 512
+GROUPS = 4
+
+NAMES = ("f1", "i1", "c1", "o1", "f2", "i2", "c2", "o2")
+ORDER = ("f1", "f2", "i1", "c1", "i2", "c2", "o1", "o2")
+LAST = "o2"
+LAST_CHUNKS = ((0, 256), (256, 512), (512, 768), (768, 1024))
+
+FLOPS = 2 * 128 * 2048 * 8192
+BYTES = 8 * (2048 * 1024 + 64 * 1024 + 2 * 1024) + 4 * 128 * 1024 * 2 + 2 * 128 * 1024 * 4
+
+
+def tile_customlstmcell_w_kernel(tc, y, h_light, c_light, h_temp, c_temp, *rest):
+    nc = tc.nc
+    words = {}
+    scales = {}
+    biases = {}
+    row_of = {}
+    for i, name in enumerate(NAMES):
+        words[name] = rest[3 * i]
+        scales[name] = rest[3 * i + 1]
+        biases[name] = rest[3 * i + 2]
+        row_of[name] = i
+    h_new = rest[24]
+    c_new = rest[25]
+
+    with ExitStack() as ctx:
+        keep = ctx.enter_context(tc.tile_pool(name="keep", bufs=1))
+        psum = ctx.enter_context(tc.psum_pool(name="psum", bufs=8))
+        ctx.enter_context(tc.manual_schedule())
+
+        bias_rows = keep.tile([P, H], BF16, name="bias_rows")
+        nc.vector.memset(bias_rows[:], 0.0)
+        planes = {}
+        for name in ORDER:
+            planes[name] = keep.tile([P, H], U8, name="plane_" + name, align_bytes=64)
+            nc.vector.memset(planes[name][:].bitcast(I32), 0)
+
+        ident_f32 = keep.tile([P, P], F32, name="ident_f32")
+        make_identity(nc, ident_f32[:])
+        ident_bf16 = keep.tile([P, P], BF16, name="ident_bf16")
+        make_identity(nc, ident_bf16[:])
+        for name in ORDER:
+            r = row_of[name]
+            nc.gpsimd.dma_start(out=bias_rows[r : r + 1, :], in_=biases[name].unsqueeze(0))
+
+        x_in = {}
+        for xname, src in (("h1", h_light), ("y", y), ("h2", h_temp)):
+            x_in[xname] = keep.tile([P, H], BF16, name="x_" + xname)
+            nc.sync.dma_start(out=x_in[xname][:], in_=src)
+        c_in = keep.tile([P, H], BF16, name="c_in")
+
+        w_tiles = {}
+        for name in ORDER:
+            for q in range(4):
+                nc.sync.dma_start(
+                    out=planes[name][32 * q : 32 * q + 16, :].bitcast(I32),
+                    in_=scales[name][:, 4 * q : 4 * q + 4, :].bitcast(I32),
+                )
+            if name == LAST:
+                for c0, c1 in LAST_CHUNKS:
+                    wt = keep.tile([P, GROUPS, c1 - c0], U32, name="w_%s_%d" % (name, c0), align_bytes=64)
+                    nc.sync.dma_start(
+                        out=wt[:].bitcast(I32),
+                        in_=words[name][:, :, c0:c1, :].rearrange("g p n t -> p g (n t)").bitcast(I32),
+                    )
+                    w_tiles[(name, c0)] = wt
+            else:
+                for j in range(2):
+                    wt = keep.tile([P, 2, H], U32, name="w_%s_%d" % (name, j), align_bytes=64)
+                    nc.sync.dma_start(
+                        out=wt[:].bitcast(I32),
+                        in_=words[name][2 * j : 2 * j + 2].rearrange("g p n t -> p g (n t)").bitcast(I32),
+                    )
+                    w_tiles[(name, j)] = wt
+            if name == ORDER[0]:
+                nc.sync.dma_start(out=c_in[:], in_=c_light)
+
+        x_t = {}
+        for xname in ("h1", "y", "h2"):
+            x_t[xname] = psum.tile([P, 2, 2, P], F32, name="xt_" + xname, tag="bank")
+            x_words = x_in[xname][:].bitcast(F32)
+            for gl in range(2):
+                for u in range(2):
+                    nc.tensor.transpose(
+                        x_t[xname][:, gl, u, :],
+                        x_words[:, 256 * gl + u : 256 * (gl + 1) : 2],
+                        ident_f32[:],
+                    )
+        grouped = {}
+        for xname in ("h1", "y", "h2"):
+            grouped[xname] = keep.tile([P, 2, P, 4], BF16, name="grouped_" + xname, align_bytes=64)
+            src = x_t[xname][:].rearrange("p g u m -> p g m u")
+            if xname == "y":
+                nc.scalar.copy(out=grouped[xname][:].bitcast(F32), in_=src)
+            else:
+                nc.vector.tensor_copy(out=grouped[xname][:].bitcast(F32), in_=src)
+        x_codes = {}
+        x_scales = {}
+        for xname in ("h1", "y", "h2"):
+            x_codes[xname] = keep.tile([P, 2 * P], U32, name="xc_" + xname, align_bytes=64)
+            x_scales[xname] = keep.tile([P, 2 * P], U8, name="xs_" + xname, align_bytes=64)
+            nc.vector.quantize_mx(
+                out=x_codes[xname][:].bitcast(FP8X4),
+                scales=x_scales[xname][:],
+                in_=grouped[xname][:].rearrange("p g m t -> p (g m t)"),
+            )
+
+        bias_bc = {}
+
+        def broadcast_bias(name):
+            r = row_of[name]
+            bb = psum.tile([P, H], BF16, name="bb_" + name, tag="bank")
+            for h in range(2):
+                nc.tensor.matmul(
+                    out=bb[:, BANK * h : BANK * (h + 1)],
+                    lhsT=ident_bf16[:, r : r + 1].to_broadcast([P, P]),
+                    rhs=bias_rows[:, BANK * h : BANK * (h + 1)],
+                    start=True,
+                    stop=True,
+                )
+            bias_bc[name] = keep.tile([P, H], BF16, name="bias_" + name)
+            nc.scalar.copy(out=bias_bc[name][:], in_=bb[:])
+
+        def mx_pass(out, name, g, rhs, c0, c1):
+            xname = ("h1" if name[1] == "1" else "h2") if g < 2 else "y"
+            gl = g % 2
+            nc.tensor.matmul_mx(
+                out=out,
+                lhsT=x_codes[xname][:, P * gl : P * (gl + 1)].bitcast(FP8X4),
+                lhsT_scale=x_scales[xname][:, P * gl : P * (gl + 1)],
+                rhs=rhs.bitcast(FP8X4),
+                rhs_scale=planes[name][4 * g : P, c0:c1],
+                start=(g == 0),
+                stop=(g == GROUPS - 1),
+            )
+
+        broadcast_bias(ORDER[0])
+        broadcast_bias(ORDER[1])
+
+        gate = {}
+        for i, name in enumerate(ORDER):
+            if i + 2 < len(ORDER):
+                broadcast_bias(ORDER[i + 2])
+            if name == LAST:
+                break
+            z = [psum.tile([P, BANK], F32, name="z_%s_%d" % (name, h), tag="bank") for h in range(2)]
+            for g in range(GROUPS):
+                for h in range(2):
+                    mx_pass(
+                        z[h][:], name, g,
+                        w_tiles[(name, g // 2)][:, g % 2, BANK * h : BANK * (h + 1)],
+                        BANK * h, BANK * (h + 1),
+                    )
+            gate[name] = keep.tile([P, H], F32, name="gate_" + name)
+            for h in range(2):
+                cols = slice(BANK * h, BANK * (h + 1))
+                nc.vector.tensor_tensor(out=gate[name][:, cols], in0=z[h][:], in1=bias_bc[name][:, cols], op=ALU.add)
+            nc.scalar.activation(
+                out=gate[name][:], in_=gate[name][:], func=ACT.Tanh, scale=(1.0 if name[0] == "c" else 0.5)
+            )
+            if name == "f2":
+                nc.vector.scalar_tensor_tensor(
+                    out=gate["f1"][:], in0=gate["f1"][:], scalar=2.0, in1=gate["f2"][:], op0=ALU.add, op1=ALU.add
+                )
+                nc.vector.scalar_tensor_tensor(
+                    out=gate["f2"][:], in0=gate["f1"][:], scalar=0.5, in1=c_in[:], op0=ALU.mult, op1=ALU.mult
+                )
+            if name == "c1":
+                nc.vector.scalar_tensor_tensor(
+                    out=gate["i1"][:], in0=gate["i1"][:], scalar=1.0, in1=gate["c1"][:], op0=ALU.add, op1=ALU.mult
+                )
+            if name == "c2":
+                nc.vector.scalar_tensor_tensor(
+                    out=gate["i2"][:], in0=gate["i2"][:], scalar=1.0, in1=gate["c2"][:], op0=ALU.add, op1=ALU.mult
+                )
+                nc.vector.tensor_tensor(out=gate["i1"][:], in0=gate["i1"][:], in1=gate["i2"][:], op=ALU.add)
+                nc.vector.scalar_tensor_tensor(
+                    out=gate["c1"][:], in0=gate["i1"][:], scalar=0.5, in1=gate["f2"][:], op0=ALU.mult, op1=ALU.add
+                )
+                nc.scalar.activation(out=gate["c2"][:], in_=gate["c1"][:], func=ACT.Tanh)
+                nc.sync.dma_start(out=c_new, in_=gate["c1"][:])
+            if name == "o1":
+                nc.vector.tensor_scalar(
+                    out=gate["o1"][:], in0=gate["o1"][:], scalar1=0.5, scalar2=1.0, op0=ALU.mult, op1=ALU.add
+                )
+
+        tanh_c = gate["c2"]
+        o1_part = gate["o1"]
+        for c0, c1 in LAST_CHUNKS:
+            n = c1 - c0
+            z = psum.tile([P, BANK], F32, name="z_last_%d" % c0, tag="bank")
+            for g in range(GROUPS):
+                mx_pass(z[:, :n], LAST, g, w_tiles[(LAST, c0)][:, g, :], c0, c1)
+            a = keep.tile([P, n], F32, name="last_%d" % c0)
+            nc.vector.tensor_tensor(out=a[:], in0=z[:, :n], in1=bias_bc[LAST][:, c0:c1], op=ALU.add)
+            nc.scalar.activation(out=a[:], in_=a[:], func=ACT.Tanh, scale=0.5)
+            nc.vector.scalar_tensor_tensor(
+                out=a[:], in0=a[:], scalar=0.5, in1=o1_part[:, c0:c1], op0=ALU.mult, op1=ALU.add
+            )
+            nc.vector.tensor_tensor(out=a[:], in0=a[:], in1=tanh_c[:, c0:c1], op=ALU.mult)
+            nc.sync.dma_start(out=h_new[:, c0:c1], in_=a[:])

@@ -21,6 +21,7 @@ NAMES = ("f1", "i1", "c1", "o1", "f2", "i2", "c2", "o2")
 ORDER = ("f1", "f2", "i1", "c1", "i2", "c2", "o1", "o2")
 LAST = "o2"
 LAST_CHUNKS = ((0, 256), (256, 512), (512, 768), (768, 1024))
+X_NAMES = ("h1", "y", "h2")
 
 FLOPS = 2 * 128 * 2048 * 8192
 BYTES = 8 * (2048 * 1024 + 64 * 1024 + 2 * 1024) + 4 * 128 * 1024 * 2 + 2 * 128 * 1024 * 4
@@ -45,20 +46,47 @@ def tile_customlstmcell_w_kernel(tc, y, h_light, c_light, h_temp, c_temp, *rest)
         psum = ctx.enter_context(tc.psum_pool(name="psum", bufs=8))
         ctx.enter_context(tc.manual_schedule())
 
-        bias_rows = keep.tile([P, H], BF16, name="bias_rows")
-        nc.vector.memset(bias_rows[:], 0.0)
         planes = {}
         for name in ORDER:
             planes[name] = keep.tile([P, H], U8, name="plane_" + name, align_bytes=64)
+        bias_rows = keep.tile([P, H], BF16, name="bias_rows")
+        nc.vector.memset(planes[ORDER[0]][:].bitcast(I32), 0)
+        nc.vector.memset(bias_rows[:], 0.0)
+        for name in ORDER[1:]:
             nc.vector.memset(planes[name][:].bitcast(I32), 0)
-
         ident_f32 = keep.tile([P, P], F32, name="ident_f32")
         make_identity(nc, ident_f32[:])
         ident_bf16 = keep.tile([P, P], BF16, name="ident_bf16")
-        make_identity(nc, ident_bf16[:])
-        for name in ORDER:
+        nc.vector.tensor_copy(out=ident_bf16[:], in_=ident_f32[:])
+
+        w_tiles = {}
+
+        def load_scales(name):
+            for q in range(4):
+                nc.sync.dma_start(
+                    out=planes[name][32 * q : 32 * q + 16, :].bitcast(I32),
+                    in_=scales[name][:, 4 * q : 4 * q + 4, :].bitcast(I32),
+                )
+
+        def load_half(name, j):
+            wt = keep.tile([P, 2, H], U32, name="w_%s_%d" % (name, j), align_bytes=64)
+            nc.sync.dma_start(
+                out=wt[:].bitcast(I32),
+                in_=words[name][2 * j : 2 * j + 2].rearrange("g p n t -> p g (n t)").bitcast(I32),
+            )
+            w_tiles[(name, j)] = wt
+
+        def load_chunk(name, c0, c1):
+            wt = keep.tile([P, GROUPS, c1 - c0], U32, name="w_%s_%d" % (name, c0), align_bytes=64)
+            nc.sync.dma_start(
+                out=wt[:].bitcast(I32),
+                in_=words[name][:, :, c0:c1, :].rearrange("g p n t -> p g (n t)").bitcast(I32),
+            )
+            w_tiles[(name, c0)] = wt
+
+        def load_bias(name):
             r = row_of[name]
-            nc.gpsimd.dma_start(out=bias_rows[r : r + 1, :], in_=biases[name].unsqueeze(0))
+            nc.sync.dma_start(out=bias_rows[r : r + 1, :], in_=biases[name].unsqueeze(0))
 
         x_in = {}
         for xname, src in (("h1", h_light), ("y", y), ("h2", h_temp)):
@@ -66,34 +94,27 @@ def tile_customlstmcell_w_kernel(tc, y, h_light, c_light, h_temp, c_temp, *rest)
             nc.sync.dma_start(out=x_in[xname][:], in_=src)
         c_in = keep.tile([P, H], BF16, name="c_in")
 
-        w_tiles = {}
-        for name in ORDER:
-            for q in range(4):
-                nc.sync.dma_start(
-                    out=planes[name][32 * q : 32 * q + 16, :].bitcast(I32),
-                    in_=scales[name][:, 4 * q : 4 * q + 4, :].bitcast(I32),
-                )
+        load_scales(ORDER[0])
+        load_half(ORDER[0], 0)
+        load_bias(ORDER[0])
+        load_half(ORDER[0], 1)
+        load_bias(ORDER[1])
+        load_bias(ORDER[2])
+        nc.sync.dma_start(out=c_in[:], in_=c_light)
+        for i in range(1, len(ORDER)):
+            name = ORDER[i]
+            load_scales(name)
             if name == LAST:
                 for c0, c1 in LAST_CHUNKS:
-                    wt = keep.tile([P, GROUPS, c1 - c0], U32, name="w_%s_%d" % (name, c0), align_bytes=64)
-                    nc.sync.dma_start(
-                        out=wt[:].bitcast(I32),
-                        in_=words[name][:, :, c0:c1, :].rearrange("g p n t -> p g (n t)").bitcast(I32),
-                    )
-                    w_tiles[(name, c0)] = wt
+                    load_chunk(name, c0, c1)
             else:
-                for j in range(2):
-                    wt = keep.tile([P, 2, H], U32, name="w_%s_%d" % (name, j), align_bytes=64)
-                    nc.sync.dma_start(
-                        out=wt[:].bitcast(I32),
-                        in_=words[name][2 * j : 2 * j + 2].rearrange("g p n t -> p g (n t)").bitcast(I32),
-                    )
-                    w_tiles[(name, j)] = wt
-            if name == ORDER[0]:
-                nc.sync.dma_start(out=c_in[:], in_=c_light)
+                load_half(name, 0)
+                load_half(name, 1)
+            if i + 2 < len(ORDER):
+                load_bias(ORDER[i + 2])
 
         x_t = {}
-        for xname in ("h1", "y", "h2"):
+        for xname in X_NAMES:
             x_t[xname] = psum.tile([P, 2, 2, P], F32, name="xt_" + xname, tag="bank")
             x_words = x_in[xname][:].bitcast(F32)
             for gl in range(2):
@@ -104,7 +125,7 @@ def tile_customlstmcell_w_kernel(tc, y, h_light, c_light, h_temp, c_temp, *rest)
                         ident_f32[:],
                     )
         grouped = {}
-        for xname in ("h1", "y", "h2"):
+        for xname in ("h1", "h2", "y"):
             grouped[xname] = keep.tile([P, 2, P, 4], BF16, name="grouped_" + xname, align_bytes=64)
             src = x_t[xname][:].rearrange("p g u m -> p g m u")
             if xname == "y":
@@ -113,7 +134,7 @@ def tile_customlstmcell_w_kernel(tc, y, h_light, c_light, h_temp, c_temp, *rest)
                 nc.vector.tensor_copy(out=grouped[xname][:].bitcast(F32), in_=src)
         x_codes = {}
         x_scales = {}
-        for xname in ("h1", "y", "h2"):
+        for xname in X_NAMES:
             x_codes[xname] = keep.tile([P, 2 * P], U32, name="xc_" + xname, align_bytes=64)
             x_scales[xname] = keep.tile([P, 2 * P], U8, name="xs_" + xname, align_bytes=64)
             nc.vector.quantize_mx(
@@ -123,6 +144,7 @@ def tile_customlstmcell_w_kernel(tc, y, h_light, c_light, h_temp, c_temp, *rest)
             )
 
         bias_bc = {}
+        gate = {}
 
         def broadcast_bias(name):
             r = row_of[name]
@@ -151,15 +173,7 @@ def tile_customlstmcell_w_kernel(tc, y, h_light, c_light, h_temp, c_temp, *rest)
                 stop=(g == GROUPS - 1),
             )
 
-        broadcast_bias(ORDER[0])
-        broadcast_bias(ORDER[1])
-
-        gate = {}
-        for i, name in enumerate(ORDER):
-            if i + 2 < len(ORDER):
-                broadcast_bias(ORDER[i + 2])
-            if name == LAST:
-                break
+        def gate_matmuls(name):
             z = [psum.tile([P, BANK], F32, name="z_%s_%d" % (name, h), tag="bank") for h in range(2)]
             for g in range(GROUPS):
                 for h in range(2):
@@ -168,6 +182,9 @@ def tile_customlstmcell_w_kernel(tc, y, h_light, c_light, h_temp, c_temp, *rest)
                         w_tiles[(name, g // 2)][:, g % 2, BANK * h : BANK * (h + 1)],
                         BANK * h, BANK * (h + 1),
                     )
+            return z
+
+        def gate_tanh(name, z):
             gate[name] = keep.tile([P, H], F32, name="gate_" + name)
             for h in range(2):
                 cols = slice(BANK * h, BANK * (h + 1))
@@ -175,25 +192,28 @@ def tile_customlstmcell_w_kernel(tc, y, h_light, c_light, h_temp, c_temp, *rest)
             nc.scalar.activation(
                 out=gate[name][:], in_=gate[name][:], func=ACT.Tanh, scale=(1.0 if name[0] == "c" else 0.5)
             )
-            if name == "f2":
-                nc.vector.scalar_tensor_tensor(
-                    out=gate["f1"][:], in0=gate["f1"][:], scalar=2.0, in1=gate["f2"][:], op0=ALU.add, op1=ALU.add
-                )
-                nc.vector.scalar_tensor_tensor(
-                    out=gate["f2"][:], in0=gate["f1"][:], scalar=0.5, in1=c_in[:], op0=ALU.mult, op1=ALU.mult
-                )
-            if name == "c1":
-                nc.vector.scalar_tensor_tensor(
-                    out=gate["i1"][:], in0=gate["i1"][:], scalar=1.0, in1=gate["c1"][:], op0=ALU.add, op1=ALU.mult
-                )
+
+        def stt(out, in0, scalar, in1, op0, op1):
+            nc.vector.scalar_tensor_tensor(out=out[:], in0=in0[:], scalar=scalar, in1=in1[:], op0=op0, op1=op1)
+
+        z = gate_matmuls(ORDER[0])
+        broadcast_bias(ORDER[0])
+        broadcast_bias(ORDER[1])
+        gate_tanh(ORDER[0], z)
+        for i in range(1, len(ORDER) - 1):
+            name = ORDER[i]
+            z = gate_matmuls(name)
+            broadcast_bias(ORDER[i + 1])
+            gate_tanh(name, z)
+            if name == "i1":
+                stt(gate["f1"], gate["f1"], 2.0, gate["f2"], ALU.add, ALU.add)
+                stt(gate["f2"], gate["f1"], 0.5, c_in, ALU.mult, ALU.mult)
+            if name == "i2":
+                stt(gate["i1"], gate["i1"], 1.0, gate["c1"], ALU.add, ALU.mult)
+                stt(gate["f2"], gate["i1"], 0.5, gate["f2"], ALU.mult, ALU.add)
             if name == "c2":
-                nc.vector.scalar_tensor_tensor(
-                    out=gate["i2"][:], in0=gate["i2"][:], scalar=1.0, in1=gate["c2"][:], op0=ALU.add, op1=ALU.mult
-                )
-                nc.vector.tensor_tensor(out=gate["i1"][:], in0=gate["i1"][:], in1=gate["i2"][:], op=ALU.add)
-                nc.vector.scalar_tensor_tensor(
-                    out=gate["c1"][:], in0=gate["i1"][:], scalar=0.5, in1=gate["f2"][:], op0=ALU.mult, op1=ALU.add
-                )
+                stt(gate["i2"], gate["i2"], 1.0, gate["c2"], ALU.add, ALU.mult)
+                stt(gate["c1"], gate["i2"], 0.5, gate["f2"], ALU.mult, ALU.add)
                 nc.scalar.activation(out=gate["c2"][:], in_=gate["c1"][:], func=ACT.Tanh)
                 nc.sync.dma_start(out=c_new, in_=gate["c1"][:])
             if name == "o1":

@@ -32,12 +32,10 @@ def tile_customlstmcell_w_kernel(tc, y, h_light, c_light, h_temp, c_temp, *rest)
     words = {}
     scales = {}
     biases = {}
-    row_of = {}
     for i, name in enumerate(NAMES):
         words[name] = rest[3 * i]
         scales[name] = rest[3 * i + 1]
         biases[name] = rest[3 * i + 2]
-        row_of[name] = i
     h_new = rest[24]
     c_new = rest[25]
 
@@ -49,13 +47,20 @@ def tile_customlstmcell_w_kernel(tc, y, h_light, c_light, h_temp, c_temp, *rest)
         planes = {}
         for name in ORDER:
             planes[name] = keep.tile([P, H], U8, name="plane_" + name, align_bytes=64)
-        bias_rows = keep.tile([P, H], BF16, name="bias_rows")
+        bias_rows = {}
         nc.vector.memset(planes[ORDER[0]][:].bitcast(I32), 0)
-        nc.vector.memset(bias_rows[:], 0.0)
+        for i in range(0, len(ORDER), 2):
+            pair = keep.tile([P, H], BF16, name="bias_rows_%d" % i)
+            nc.vector.memset(pair[:], 0.0)
+            bias_rows[ORDER[i]] = (pair, 0)
+            bias_rows[ORDER[i + 1]] = (pair, 1)
         for name in ORDER[1:]:
             nc.vector.memset(planes[name][:].bitcast(I32), 0)
         ident_f32 = keep.tile([P, P], F32, name="ident_f32")
         make_identity(nc, ident_f32[:])
+        for name in ORDER:
+            pair, r = bias_rows[name]
+            nc.gpsimd.dma_start(out=pair[r : r + 1, :], in_=biases[name].unsqueeze(0))
         ident_bf16 = keep.tile([P, P], BF16, name="ident_bf16")
         nc.vector.tensor_copy(out=ident_bf16[:], in_=ident_f32[:])
 
@@ -84,10 +89,6 @@ def tile_customlstmcell_w_kernel(tc, y, h_light, c_light, h_temp, c_temp, *rest)
             )
             w_tiles[(name, c0)] = wt
 
-        def load_bias(name):
-            r = row_of[name]
-            nc.sync.dma_start(out=bias_rows[r : r + 1, :], in_=biases[name].unsqueeze(0))
-
         x_in = {}
         for xname, src in (("h1", h_light), ("y", y), ("h2", h_temp)):
             x_in[xname] = keep.tile([P, H], BF16, name="x_" + xname)
@@ -96,10 +97,7 @@ def tile_customlstmcell_w_kernel(tc, y, h_light, c_light, h_temp, c_temp, *rest)
 
         load_scales(ORDER[0])
         load_half(ORDER[0], 0)
-        load_bias(ORDER[0])
         load_half(ORDER[0], 1)
-        load_bias(ORDER[1])
-        load_bias(ORDER[2])
         nc.sync.dma_start(out=c_in[:], in_=c_light)
         for i in range(1, len(ORDER)):
             name = ORDER[i]
@@ -110,8 +108,6 @@ def tile_customlstmcell_w_kernel(tc, y, h_light, c_light, h_temp, c_temp, *rest)
             else:
                 load_half(name, 0)
                 load_half(name, 1)
-            if i + 2 < len(ORDER):
-                load_bias(ORDER[i + 2])
 
         x_t = {}
         for xname in X_NAMES:
@@ -147,13 +143,13 @@ def tile_customlstmcell_w_kernel(tc, y, h_light, c_light, h_temp, c_temp, *rest)
         gate = {}
 
         def broadcast_bias(name):
-            r = row_of[name]
+            pair, r = bias_rows[name]
             bb = psum.tile([P, H], BF16, name="bb_" + name, tag="bank")
             for h in range(2):
                 nc.tensor.matmul(
                     out=bb[:, BANK * h : BANK * (h + 1)],
                     lhsT=ident_bf16[:, r : r + 1].to_broadcast([P, P]),
-                    rhs=bias_rows[:, BANK * h : BANK * (h + 1)],
+                    rhs=pair[:, BANK * h : BANK * (h + 1)],
                     start=True,
                     stop=True,
                 )
@@ -184,55 +180,66 @@ def tile_customlstmcell_w_kernel(tc, y, h_light, c_light, h_temp, c_temp, *rest)
                     )
             return z
 
-        def gate_tanh(name, z):
-            gate[name] = keep.tile([P, H], F32, name="gate_" + name)
-            for h in range(2):
-                cols = slice(BANK * h, BANK * (h + 1))
-                nc.vector.tensor_tensor(out=gate[name][:, cols], in0=z[h][:], in1=bias_bc[name][:, cols], op=ALU.add)
-            nc.scalar.activation(
-                out=gate[name][:], in_=gate[name][:], func=ACT.Tanh, scale=(1.0 if name[0] == "c" else 0.5)
-            )
+        def halves():
+            return [slice(BANK * h, BANK * (h + 1)) for h in range(2)]
 
-        def stt(out, in0, scalar, in1, op0, op1):
-            nc.vector.scalar_tensor_tensor(out=out[:], in0=in0[:], scalar=scalar, in1=in1[:], op0=op0, op1=op1)
+        def gate_act(name, z):
+            gate[name] = keep.tile([P, H], F32, name="gate_" + name)
+            for h, cols in enumerate(halves()):
+                nc.vector.tensor_tensor(out=gate[name][:, cols], in0=z[h][:], in1=bias_bc[name][:, cols], op=ALU.add)
+            for cols in halves():
+                nc.scalar.activation(
+                    out=gate[name][:, cols], in_=gate[name][:, cols],
+                    func=(ACT.Tanh if name[0] == "c" else ACT.Sigmoid),
+                )
+
+        def tt(out, in0, in1, op):
+            nc.vector.tensor_tensor(out=out, in0=in0, in1=in1, op=op)
 
         z = gate_matmuls(ORDER[0])
         broadcast_bias(ORDER[0])
         broadcast_bias(ORDER[1])
-        gate_tanh(ORDER[0], z)
+        gate_act(ORDER[0], z)
         for i in range(1, len(ORDER) - 1):
             name = ORDER[i]
             z = gate_matmuls(name)
             broadcast_bias(ORDER[i + 1])
-            gate_tanh(name, z)
+            gate_act(name, z)
             if name == "i1":
-                stt(gate["f1"], gate["f1"], 2.0, gate["f2"], ALU.add, ALU.add)
-                stt(gate["f2"], gate["f1"], 0.5, c_in, ALU.mult, ALU.mult)
+                tt(gate["f1"][:], gate["f1"][:], gate["f2"][:], ALU.add)
+                tt(gate["f2"][:], gate["f1"][:], c_in[:], ALU.mult)
             if name == "i2":
-                stt(gate["i1"], gate["i1"], 1.0, gate["c1"], ALU.add, ALU.mult)
-                stt(gate["f2"], gate["i1"], 0.5, gate["f2"], ALU.mult, ALU.add)
+                tt(gate["i1"][:], gate["i1"][:], gate["c1"][:], ALU.mult)
+                tt(gate["f2"][:], gate["i1"][:], gate["f2"][:], ALU.add)
             if name == "c2":
-                stt(gate["i2"], gate["i2"], 1.0, gate["c2"], ALU.add, ALU.mult)
-                stt(gate["c1"], gate["i2"], 0.5, gate["f2"], ALU.mult, ALU.add)
-                nc.scalar.activation(out=gate["c2"][:], in_=gate["c1"][:], func=ACT.Tanh)
+                for cols in halves():
+                    tt(gate["i2"][:, cols], gate["i2"][:, cols], gate["c2"][:, cols], ALU.mult)
+                    tt(gate["c1"][:, cols], gate["i2"][:, cols], gate["f2"][:, cols], ALU.add)
+                    nc.scalar.activation(out=gate["c2"][:, cols], in_=gate["c1"][:, cols], func=ACT.Tanh)
                 nc.sync.dma_start(out=c_new, in_=gate["c1"][:])
-            if name == "o1":
-                nc.vector.tensor_scalar(
-                    out=gate["o1"][:], in0=gate["o1"][:], scalar1=0.5, scalar2=1.0, op0=ALU.mult, op1=ALU.add
-                )
 
         tanh_c = gate["c2"]
-        o1_part = gate["o1"]
-        for c0, c1 in LAST_CHUNKS:
+        o_first = gate["o1"]
+        last = {}
+
+        def last_front(c0, c1):
             n = c1 - c0
-            z = psum.tile([P, BANK], F32, name="z_last_%d" % c0, tag="bank")
+            zl = psum.tile([P, BANK], F32, name="z_last_%d" % c0, tag="bank")
             for g in range(GROUPS):
-                mx_pass(z[:, :n], LAST, g, w_tiles[(LAST, c0)][:, g, :], c0, c1)
+                mx_pass(zl[:, :n], LAST, g, w_tiles[(LAST, c0)][:, g, :], c0, c1)
             a = keep.tile([P, n], F32, name="last_%d" % c0)
-            nc.vector.tensor_tensor(out=a[:], in0=z[:, :n], in1=bias_bc[LAST][:, c0:c1], op=ALU.add)
-            nc.scalar.activation(out=a[:], in_=a[:], func=ACT.Tanh, scale=0.5)
-            nc.vector.scalar_tensor_tensor(
-                out=a[:], in0=a[:], scalar=0.5, in1=o1_part[:, c0:c1], op0=ALU.mult, op1=ALU.add
-            )
-            nc.vector.tensor_tensor(out=a[:], in0=a[:], in1=tanh_c[:, c0:c1], op=ALU.mult)
+            tt(a[:], zl[:, :n], bias_bc[LAST][:, c0:c1], ALU.add)
+            nc.scalar.activation(out=a[:], in_=a[:], func=ACT.Sigmoid)
+            last[c0] = a
+
+        def last_back(c0, c1):
+            a = last[c0]
+            tt(a[:], a[:], o_first[:, c0:c1], ALU.add)
+            tt(a[:], a[:], tanh_c[:, c0:c1], ALU.mult)
             nc.sync.dma_start(out=h_new[:, c0:c1], in_=a[:])
+
+        for k, (c0, c1) in enumerate(LAST_CHUNKS):
+            last_front(c0, c1)
+            if k > 0:
+                last_back(*LAST_CHUNKS[k - 1])
+        last_back(*LAST_CHUNKS[-1])

@@ -58,9 +58,26 @@ def tile_customlstmcell_w_kernel(tc, y, h_light, c_light, h_temp, c_temp, *rest)
             nc.vector.memset(planes[name][:].bitcast(I32), 0)
         ident_f32 = keep.tile([P, P], F32, name="ident_f32")
         make_identity(nc, ident_f32[:])
-        for name in ORDER:
+
+        def load_bias(name):
             pair, r = bias_rows[name]
             nc.gpsimd.dma_start(out=pair[r : r + 1, :], in_=biases[name].unsqueeze(0))
+
+        def load_scales_soft(name):
+            for q in range(4):
+                nc.gpsimd.dma_start(
+                    out=planes[name][32 * q : 32 * q + 16, :].bitcast(F32),
+                    in_=scales[name][:, 4 * q : 4 * q + 4, :].bitcast(F32),
+                )
+
+        for name in ORDER[:4]:
+            load_bias(name)
+        for i in range(2, len(ORDER), 2):
+            load_scales_soft(ORDER[i])
+            load_scales_soft(ORDER[i + 1])
+            if i + 2 < len(ORDER):
+                load_bias(ORDER[i + 2])
+                load_bias(ORDER[i + 3])
         ident_bf16 = keep.tile([P, P], BF16, name="ident_bf16")
         nc.vector.tensor_copy(out=ident_bf16[:], in_=ident_f32[:])
 
@@ -101,7 +118,8 @@ def tile_customlstmcell_w_kernel(tc, y, h_light, c_light, h_temp, c_temp, *rest)
         nc.sync.dma_start(out=c_in[:], in_=c_light)
         for i in range(1, len(ORDER)):
             name = ORDER[i]
-            load_scales(name)
+            if i < 2:
+                load_scales(name)
             if name == LAST:
                 for c0, c1 in LAST_CHUNKS:
                     load_chunk(name, c0, c1)

@@ -20,7 +20,7 @@ GROUPS = 4
 NAMES = ("f1", "i1", "c1", "o1", "f2", "i2", "c2", "o2")
 ORDER = ("f1", "f2", "i1", "c1", "i2", "c2", "o1", "o2")
 LAST = "o2"
-LAST_CHUNKS = ((0, 256), (256, 512), (512, 768), (768, 1024))
+LAST_CHUNKS = ((0, 256), (256, 512), (512, 768), (768, 896), (896, 1024))
 X_NAMES = ("h1", "y", "h2")
 
 FLOPS = 2 * 128 * 2048 * 8192
@@ -45,50 +45,40 @@ def tile_customlstmcell_w_kernel(tc, y, h_light, c_light, h_temp, c_temp, *rest)
         ctx.enter_context(tc.manual_schedule())
 
         planes = {}
-        for name in ORDER:
-            planes[name] = keep.tile([P, H], U8, name="plane_" + name, align_bytes=64)
         bias_rows = {}
-        nc.vector.memset(planes[ORDER[0]][:].bitcast(I32), 0)
         for i in range(0, len(ORDER), 2):
+            for name in ORDER[i : i + 2]:
+                planes[name] = keep.tile([P, H], U8, name="plane_" + name, align_bytes=64)
+                nc.vector.memset(planes[name][:].bitcast(I32), 0)
             pair = keep.tile([P, H], BF16, name="bias_rows_%d" % i)
             nc.vector.memset(pair[:], 0.0)
             bias_rows[ORDER[i]] = (pair, 0)
             bias_rows[ORDER[i + 1]] = (pair, 1)
-        for name in ORDER[1:]:
-            nc.vector.memset(planes[name][:].bitcast(I32), 0)
         ident_f32 = keep.tile([P, P], F32, name="ident_f32")
         make_identity(nc, ident_f32[:])
+        ident_bf16 = keep.tile([P, P], BF16, name="ident_bf16")
+        nc.vector.tensor_copy(out=ident_bf16[:], in_=ident_f32[:])
 
         def load_bias(name):
             pair, r = bias_rows[name]
             nc.gpsimd.dma_start(out=pair[r : r + 1, :], in_=biases[name].unsqueeze(0))
 
-        def load_scales_soft(name):
+        def load_scales(name):
             for q in range(4):
                 nc.gpsimd.dma_start(
                     out=planes[name][32 * q : 32 * q + 16, :].bitcast(F32),
                     in_=scales[name][:, 4 * q : 4 * q + 4, :].bitcast(F32),
                 )
 
-        for name in ORDER[:4]:
-            load_bias(name)
-        for i in range(2, len(ORDER), 2):
-            load_scales_soft(ORDER[i])
-            load_scales_soft(ORDER[i + 1])
+        load_scales(ORDER[0])
+        for i in range(0, len(ORDER), 2):
+            load_bias(ORDER[i])
+            load_bias(ORDER[i + 1])
+            load_scales(ORDER[i + 1])
             if i + 2 < len(ORDER):
-                load_bias(ORDER[i + 2])
-                load_bias(ORDER[i + 3])
-        ident_bf16 = keep.tile([P, P], BF16, name="ident_bf16")
-        nc.vector.tensor_copy(out=ident_bf16[:], in_=ident_f32[:])
+                load_scales(ORDER[i + 2])
 
         w_tiles = {}
-
-        def load_scales(name):
-            for q in range(4):
-                nc.sync.dma_start(
-                    out=planes[name][32 * q : 32 * q + 16, :].bitcast(I32),
-                    in_=scales[name][:, 4 * q : 4 * q + 4, :].bitcast(I32),
-                )
 
         def load_half(name, j):
             wt = keep.tile([P, 2, H], U32, name="w_%s_%d" % (name, j), align_bytes=64)
@@ -111,21 +101,15 @@ def tile_customlstmcell_w_kernel(tc, y, h_light, c_light, h_temp, c_temp, *rest)
             x_in[xname] = keep.tile([P, H], BF16, name="x_" + xname)
             nc.sync.dma_start(out=x_in[xname][:], in_=src)
         c_in = keep.tile([P, H], BF16, name="c_in")
-
-        load_scales(ORDER[0])
-        load_half(ORDER[0], 0)
-        load_half(ORDER[0], 1)
-        nc.sync.dma_start(out=c_in[:], in_=c_light)
-        for i in range(1, len(ORDER)):
-            name = ORDER[i]
-            if i < 2:
-                load_scales(name)
+        for name in ORDER:
             if name == LAST:
                 for c0, c1 in LAST_CHUNKS:
                     load_chunk(name, c0, c1)
             else:
                 load_half(name, 0)
                 load_half(name, 1)
+            if name == ORDER[0]:
+                nc.sync.dma_start(out=c_in[:], in_=c_light)
 
         x_t = {}
         for xname in X_NAMES:
@@ -198,21 +182,18 @@ def tile_customlstmcell_w_kernel(tc, y, h_light, c_light, h_temp, c_temp, *rest)
                     )
             return z
 
-        def halves():
-            return [slice(BANK * h, BANK * (h + 1)) for h in range(2)]
-
-        def gate_act(name, z):
-            gate[name] = keep.tile([P, H], F32, name="gate_" + name)
-            for h, cols in enumerate(halves()):
-                nc.vector.tensor_tensor(out=gate[name][:, cols], in0=z[h][:], in1=bias_bc[name][:, cols], op=ALU.add)
-            for cols in halves():
-                nc.scalar.activation(
-                    out=gate[name][:, cols], in_=gate[name][:, cols],
-                    func=(ACT.Tanh if name[0] == "c" else ACT.Sigmoid),
-                )
-
         def tt(out, in0, in1, op):
             nc.vector.tensor_tensor(out=out, in0=in0, in1=in1, op=op)
+
+        def gate_act(name, z):
+            for h in range(2):
+                gate[(name, h)] = keep.tile([P, BANK], F32, name="gate_%s_%d" % (name, h))
+                tt(gate[(name, h)][:], z[h][:], bias_bc[name][:, BANK * h : BANK * (h + 1)], ALU.add)
+            for h in range(2):
+                nc.scalar.activation(
+                    out=gate[(name, h)][:], in_=gate[(name, h)][:],
+                    func=(ACT.Tanh if name[0] == "c" else ACT.Sigmoid),
+                )
 
         z = gate_matmuls(ORDER[0])
         broadcast_bias(ORDER[0])
@@ -223,21 +204,19 @@ def tile_customlstmcell_w_kernel(tc, y, h_light, c_light, h_temp, c_temp, *rest)
             z = gate_matmuls(name)
             broadcast_bias(ORDER[i + 1])
             gate_act(name, z)
-            if name == "i1":
-                tt(gate["f1"][:], gate["f1"][:], gate["f2"][:], ALU.add)
-                tt(gate["f2"][:], gate["f1"][:], c_in[:], ALU.mult)
-            if name == "i2":
-                tt(gate["i1"][:], gate["i1"][:], gate["c1"][:], ALU.mult)
-                tt(gate["f2"][:], gate["i1"][:], gate["f2"][:], ALU.add)
-            if name == "c2":
-                for cols in halves():
-                    tt(gate["i2"][:, cols], gate["i2"][:, cols], gate["c2"][:, cols], ALU.mult)
-                    tt(gate["c1"][:, cols], gate["i2"][:, cols], gate["f2"][:, cols], ALU.add)
-                    nc.scalar.activation(out=gate["c2"][:, cols], in_=gate["c1"][:, cols], func=ACT.Tanh)
-                nc.sync.dma_start(out=c_new, in_=gate["c1"][:])
+            for h in range(2):
+                if name == "i1":
+                    tt(gate[("f1", h)][:], gate[("f1", h)][:], gate[("f2", h)][:], ALU.add)
+                    tt(gate[("f2", h)][:], gate[("f1", h)][:], c_in[:, BANK * h : BANK * (h + 1)], ALU.mult)
+                if name == "i2":
+                    tt(gate[("i1", h)][:], gate[("i1", h)][:], gate[("c1", h)][:], ALU.mult)
+                    tt(gate[("f2", h)][:], gate[("i1", h)][:], gate[("f2", h)][:], ALU.add)
+                if name == "c2":
+                    tt(gate[("i2", h)][:], gate[("i2", h)][:], gate[("c2", h)][:], ALU.mult)
+                    tt(gate[("c1", h)][:], gate[("i2", h)][:], gate[("f2", h)][:], ALU.add)
+                    nc.scalar.activation(out=gate[("c2", h)][:], in_=gate[("c1", h)][:], func=ACT.Tanh)
+                    nc.sync.dma_start(out=c_new[:, BANK * h : BANK * (h + 1)], in_=gate[("c1", h)][:])
 
-        tanh_c = gate["c2"]
-        o_first = gate["o1"]
         last = {}
 
         def last_front(c0, c1):
@@ -252,8 +231,10 @@ def tile_customlstmcell_w_kernel(tc, y, h_light, c_light, h_temp, c_temp, *rest)
 
         def last_back(c0, c1):
             a = last[c0]
-            tt(a[:], a[:], o_first[:, c0:c1], ALU.add)
-            tt(a[:], a[:], tanh_c[:, c0:c1], ALU.mult)
+            h = c0 // BANK
+            cols = slice(c0 - BANK * h, c1 - BANK * h)
+            tt(a[:], a[:], gate[("o1", h)][:, cols], ALU.add)
+            tt(a[:], a[:], gate[("c2", h)][:, cols], ALU.mult)
             nc.sync.dma_start(out=h_new[:, c0:c1], in_=a[:])
 
         for k, (c0, c1) in enumerate(LAST_CHUNKS):

@@ -20,7 +20,7 @@ GROUPS = 4
 NAMES = ("f1", "i1", "c1", "o1", "f2", "i2", "c2", "o2")
 ORDER = ("f1", "f2", "i1", "c1", "i2", "c2", "o1", "o2")
 LAST = "o2"
-LAST_CHUNKS = ((0, 256), (256, 512), (512, 768), (768, 896), (896, 1024))
+LAST_CHUNKS = ((0, 256), (256, 512), (512, 768), (768, 1024))
 X_NAMES = ("h1", "y", "h2")
 
 FLOPS = 2 * 128 * 2048 * 8192
@@ -56,27 +56,22 @@ def tile_customlstmcell_w_kernel(tc, y, h_light, c_light, h_temp, c_temp, *rest)
             bias_rows[ORDER[i + 1]] = (pair, 1)
         ident_f32 = keep.tile([P, P], F32, name="ident_f32")
         make_identity(nc, ident_f32[:])
-        ident_bf16 = keep.tile([P, P], BF16, name="ident_bf16")
-        nc.vector.tensor_copy(out=ident_bf16[:], in_=ident_f32[:])
 
         def load_bias(name):
             pair, r = bias_rows[name]
-            nc.gpsimd.dma_start(out=pair[r : r + 1, :], in_=biases[name].unsqueeze(0))
+            nc.sync.dma_start(out=pair[r : r + 1, :], in_=biases[name].unsqueeze(0))
 
-        def load_scales(name):
+        def load_scales_soft(name):
             for q in range(4):
                 nc.gpsimd.dma_start(
                     out=planes[name][32 * q : 32 * q + 16, :].bitcast(F32),
                     in_=scales[name][:, 4 * q : 4 * q + 4, :].bitcast(F32),
                 )
 
-        load_scales(ORDER[0])
-        for i in range(0, len(ORDER), 2):
-            load_bias(ORDER[i])
-            load_bias(ORDER[i + 1])
-            load_scales(ORDER[i + 1])
-            if i + 2 < len(ORDER):
-                load_scales(ORDER[i + 2])
+        for name in ORDER:
+            load_scales_soft(name)
+        ident_bf16 = keep.tile([P, P], BF16, name="ident_bf16")
+        nc.vector.tensor_copy(out=ident_bf16[:], in_=ident_f32[:])
 
         w_tiles = {}
 
@@ -101,15 +96,23 @@ def tile_customlstmcell_w_kernel(tc, y, h_light, c_light, h_temp, c_temp, *rest)
             x_in[xname] = keep.tile([P, H], BF16, name="x_" + xname)
             nc.sync.dma_start(out=x_in[xname][:], in_=src)
         c_in = keep.tile([P, H], BF16, name="c_in")
-        for name in ORDER:
+
+        load_half(ORDER[0], 0)
+        load_bias(ORDER[0])
+        load_bias(ORDER[1])
+        load_half(ORDER[0], 1)
+        nc.sync.dma_start(out=c_in[:], in_=c_light)
+        for i in range(1, len(ORDER)):
+            name = ORDER[i]
             if name == LAST:
                 for c0, c1 in LAST_CHUNKS:
                     load_chunk(name, c0, c1)
             else:
                 load_half(name, 0)
                 load_half(name, 1)
-            if name == ORDER[0]:
-                nc.sync.dma_start(out=c_in[:], in_=c_light)
+            if i % 2 == 1 and i + 2 < len(ORDER):
+                load_bias(ORDER[i + 1])
+                load_bias(ORDER[i + 2])
 
         x_t = {}
         for xname in X_NAMES:
@@ -182,18 +185,21 @@ def tile_customlstmcell_w_kernel(tc, y, h_light, c_light, h_temp, c_temp, *rest)
                     )
             return z
 
-        def tt(out, in0, in1, op):
-            nc.vector.tensor_tensor(out=out, in0=in0, in1=in1, op=op)
+        def halves():
+            return [slice(BANK * h, BANK * (h + 1)) for h in range(2)]
 
         def gate_act(name, z):
-            for h in range(2):
-                gate[(name, h)] = keep.tile([P, BANK], F32, name="gate_%s_%d" % (name, h))
-                tt(gate[(name, h)][:], z[h][:], bias_bc[name][:, BANK * h : BANK * (h + 1)], ALU.add)
-            for h in range(2):
+            gate[name] = keep.tile([P, H], F32, name="gate_" + name)
+            for h, cols in enumerate(halves()):
+                nc.vector.tensor_tensor(out=gate[name][:, cols], in0=z[h][:], in1=bias_bc[name][:, cols], op=ALU.add)
+            for cols in halves():
                 nc.scalar.activation(
-                    out=gate[(name, h)][:], in_=gate[(name, h)][:],
+                    out=gate[name][:, cols], in_=gate[name][:, cols],
                     func=(ACT.Tanh if name[0] == "c" else ACT.Sigmoid),
                 )
+
+        def tt(out, in0, in1, op):
+            nc.vector.tensor_tensor(out=out, in0=in0, in1=in1, op=op)
 
         z = gate_matmuls(ORDER[0])
         broadcast_bias(ORDER[0])
@@ -204,19 +210,21 @@ def tile_customlstmcell_w_kernel(tc, y, h_light, c_light, h_temp, c_temp, *rest)
             z = gate_matmuls(name)
             broadcast_bias(ORDER[i + 1])
             gate_act(name, z)
-            for h in range(2):
-                if name == "i1":
-                    tt(gate[("f1", h)][:], gate[("f1", h)][:], gate[("f2", h)][:], ALU.add)
-                    tt(gate[("f2", h)][:], gate[("f1", h)][:], c_in[:, BANK * h : BANK * (h + 1)], ALU.mult)
-                if name == "i2":
-                    tt(gate[("i1", h)][:], gate[("i1", h)][:], gate[("c1", h)][:], ALU.mult)
-                    tt(gate[("f2", h)][:], gate[("i1", h)][:], gate[("f2", h)][:], ALU.add)
-                if name == "c2":
-                    tt(gate[("i2", h)][:], gate[("i2", h)][:], gate[("c2", h)][:], ALU.mult)
-                    tt(gate[("c1", h)][:], gate[("i2", h)][:], gate[("f2", h)][:], ALU.add)
-                    nc.scalar.activation(out=gate[("c2", h)][:], in_=gate[("c1", h)][:], func=ACT.Tanh)
-                    nc.sync.dma_start(out=c_new[:, BANK * h : BANK * (h + 1)], in_=gate[("c1", h)][:])
+            if name == "i1":
+                tt(gate["f1"][:], gate["f1"][:], gate["f2"][:], ALU.add)
+                tt(gate["f2"][:], gate["f1"][:], c_in[:], ALU.mult)
+            if name == "i2":
+                tt(gate["i1"][:], gate["i1"][:], gate["c1"][:], ALU.mult)
+                tt(gate["f2"][:], gate["i1"][:], gate["f2"][:], ALU.add)
+            if name == "c2":
+                for cols in halves():
+                    tt(gate["i2"][:, cols], gate["i2"][:, cols], gate["c2"][:, cols], ALU.mult)
+                    tt(gate["c1"][:, cols], gate["i2"][:, cols], gate["f2"][:, cols], ALU.add)
+                    nc.scalar.activation(out=gate["c2"][:, cols], in_=gate["c1"][:, cols], func=ACT.Tanh)
+                nc.sync.dma_start(out=c_new, in_=gate["c1"][:])
 
+        tanh_c = gate["c2"]
+        o_first = gate["o1"]
         last = {}
 
         def last_front(c0, c1):
@@ -231,10 +239,8 @@ def tile_customlstmcell_w_kernel(tc, y, h_light, c_light, h_temp, c_temp, *rest)
 
         def last_back(c0, c1):
             a = last[c0]
-            h = c0 // BANK
-            cols = slice(c0 - BANK * h, c1 - BANK * h)
-            tt(a[:], a[:], gate[("o1", h)][:, cols], ALU.add)
-            tt(a[:], a[:], gate[("c2", h)][:, cols], ALU.mult)
+            tt(a[:], a[:], o_first[:, c0:c1], ALU.add)
+            tt(a[:], a[:], tanh_c[:, c0:c1], ALU.mult)
             nc.sync.dma_start(out=h_new[:, c0:c1], in_=a[:])
 
         for k, (c0, c1) in enumerate(LAST_CHUNKS):

@@ -45,21 +45,23 @@ def tile_customlstmcell_w_kernel(tc, y, h_light, c_light, h_temp, c_temp, *rest)
         ctx.enter_context(tc.manual_schedule())
 
         planes = {}
+        for name in ORDER:
+            planes[name] = keep.tile([P, H], U8, name="plane_" + name, align_bytes=64)
         bias_rows = {}
+        nc.vector.memset(planes[ORDER[0]][:].bitcast(I32), 0)
         for i in range(0, len(ORDER), 2):
-            for name in ORDER[i : i + 2]:
-                planes[name] = keep.tile([P, H], U8, name="plane_" + name, align_bytes=64)
-                nc.vector.memset(planes[name][:].bitcast(I32), 0)
             pair = keep.tile([P, H], BF16, name="bias_rows_%d" % i)
             nc.vector.memset(pair[:], 0.0)
             bias_rows[ORDER[i]] = (pair, 0)
             bias_rows[ORDER[i + 1]] = (pair, 1)
+        for name in ORDER[1:]:
+            nc.vector.memset(planes[name][:].bitcast(I32), 0)
         ident_f32 = keep.tile([P, P], F32, name="ident_f32")
         make_identity(nc, ident_f32[:])
 
         def load_bias(name):
             pair, r = bias_rows[name]
-            nc.sync.dma_start(out=pair[r : r + 1, :], in_=biases[name].unsqueeze(0))
+            nc.gpsimd.dma_start(out=pair[r : r + 1, :], in_=biases[name].unsqueeze(0))
 
         def load_scales_soft(name):
             for q in range(4):
@@ -68,12 +70,25 @@ def tile_customlstmcell_w_kernel(tc, y, h_light, c_light, h_temp, c_temp, *rest)
                     in_=scales[name][:, 4 * q : 4 * q + 4, :].bitcast(F32),
                 )
 
-        for name in ORDER:
-            load_scales_soft(name)
+        for name in ORDER[:4]:
+            load_bias(name)
+        for i in range(2, len(ORDER), 2):
+            load_scales_soft(ORDER[i])
+            load_scales_soft(ORDER[i + 1])
+            if i + 2 < len(ORDER):
+                load_bias(ORDER[i + 2])
+                load_bias(ORDER[i + 3])
         ident_bf16 = keep.tile([P, P], BF16, name="ident_bf16")
         nc.vector.tensor_copy(out=ident_bf16[:], in_=ident_f32[:])
 
         w_tiles = {}
+
+        def load_scales(name):
+            for q in range(4):
+                nc.sync.dma_start(
+                    out=planes[name][32 * q : 32 * q + 16, :].bitcast(I32),
+                    in_=scales[name][:, 4 * q : 4 * q + 4, :].bitcast(I32),
+                )
 
         def load_half(name, j):
             wt = keep.tile([P, 2, H], U32, name="w_%s_%d" % (name, j), align_bytes=64)
@@ -83,12 +98,13 @@ def tile_customlstmcell_w_kernel(tc, y, h_light, c_light, h_temp, c_temp, *rest)
             )
             w_tiles[(name, j)] = wt
 
-        def load_chunk(name, c0, c1):
+        def load_chunk(name, c0, c1, cuts):
             wt = keep.tile([P, GROUPS, c1 - c0], U32, name="w_%s_%d" % (name, c0), align_bytes=64)
-            nc.sync.dma_start(
-                out=wt[:].bitcast(I32),
-                in_=words[name][:, :, c0:c1, :].rearrange("g p n t -> p g (n t)").bitcast(I32),
-            )
+            for g0, g1 in cuts:
+                nc.sync.dma_start(
+                    out=wt[:, g0:g1, :].bitcast(I32),
+                    in_=words[name][g0:g1, :, c0:c1, :].rearrange("g p n t -> p g (n t)").bitcast(I32),
+                )
             w_tiles[(name, c0)] = wt
 
         x_in = {}
@@ -97,22 +113,20 @@ def tile_customlstmcell_w_kernel(tc, y, h_light, c_light, h_temp, c_temp, *rest)
             nc.sync.dma_start(out=x_in[xname][:], in_=src)
         c_in = keep.tile([P, H], BF16, name="c_in")
 
+        load_scales(ORDER[0])
         load_half(ORDER[0], 0)
-        load_bias(ORDER[0])
-        load_bias(ORDER[1])
         load_half(ORDER[0], 1)
         nc.sync.dma_start(out=c_in[:], in_=c_light)
         for i in range(1, len(ORDER)):
             name = ORDER[i]
+            if i < 2:
+                load_scales(name)
             if name == LAST:
                 for c0, c1 in LAST_CHUNKS:
-                    load_chunk(name, c0, c1)
+                    load_chunk(name, c0, c1, ((0, 3), (3, 4)) if c1 == H else ((0, 4),))
             else:
                 load_half(name, 0)
                 load_half(name, 1)
-            if i % 2 == 1 and i + 2 < len(ORDER):
-                load_bias(ORDER[i + 1])
-                load_bias(ORDER[i + 2])
 
         x_t = {}
         for xname in X_NAMES:
@@ -204,11 +218,13 @@ def tile_customlstmcell_w_kernel(tc, y, h_light, c_light, h_temp, c_temp, *rest)
         z = gate_matmuls(ORDER[0])
         broadcast_bias(ORDER[0])
         broadcast_bias(ORDER[1])
+        broadcast_bias(ORDER[2])
         gate_act(ORDER[0], z)
         for i in range(1, len(ORDER) - 1):
             name = ORDER[i]
             z = gate_matmuls(name)
-            broadcast_bias(ORDER[i + 1])
+            if i + 2 < len(ORDER):
+                broadcast_bias(ORDER[i + 2])
             gate_act(name, z)
             if name == "i1":
                 tt(gate["f1"][:], gate["f1"][:], gate["f2"][:], ALU.add)

@@ -90,13 +90,18 @@ def tile_customlstmcell_w_kernel(tc, y, h_light, c_light, h_temp, c_temp, *rest)
                     in_=scales[name][:, 4 * q : 4 * q + 4, :].bitcast(I32),
                 )
 
-        def load_half(name, j):
-            wt = keep.tile([P, 2, H], U32, name="w_%s_%d" % (name, j), align_bytes=64)
+        def load_groups(name, g0, g1):
+            wt = keep.tile([P, g1 - g0, H], U32, name="w_%s_%d" % (name, g0), align_bytes=64)
             nc.sync.dma_start(
                 out=wt[:].bitcast(I32),
-                in_=words[name][2 * j : 2 * j + 2].rearrange("g p n t -> p g (n t)").bitcast(I32),
+                in_=words[name][g0:g1].rearrange("g p n t -> p g (n t)").bitcast(I32),
             )
-            w_tiles[(name, j)] = wt
+            for g in range(g0, g1):
+                w_tiles[(name, g)] = wt[:, g - g0, :]
+
+        def load_gate(name):
+            for g in range(GROUPS):
+                load_groups(name, g, g + 1)
 
         def load_chunk(name, c0, c1, cuts):
             wt = keep.tile([P, GROUPS, c1 - c0], U32, name="w_%s_%d" % (name, c0), align_bytes=64)
@@ -114,8 +119,7 @@ def tile_customlstmcell_w_kernel(tc, y, h_light, c_light, h_temp, c_temp, *rest)
         c_in = keep.tile([P, H], BF16, name="c_in")
 
         load_scales(ORDER[0])
-        load_half(ORDER[0], 0)
-        load_half(ORDER[0], 1)
+        load_gate(ORDER[0])
         nc.sync.dma_start(out=c_in[:], in_=c_light)
         for i in range(1, len(ORDER)):
             name = ORDER[i]
@@ -125,8 +129,7 @@ def tile_customlstmcell_w_kernel(tc, y, h_light, c_light, h_temp, c_temp, *rest)
                 for c0, c1 in LAST_CHUNKS:
                     load_chunk(name, c0, c1, ((0, 3), (3, 4)) if c1 == H else ((0, 4),))
             else:
-                load_half(name, 0)
-                load_half(name, 1)
+                load_gate(name)
 
         x_t = {}
         for xname in X_NAMES:
@@ -194,7 +197,7 @@ def tile_customlstmcell_w_kernel(tc, y, h_light, c_light, h_temp, c_temp, *rest)
                 for h in range(2):
                     mx_pass(
                         z[h][:], name, g,
-                        w_tiles[(name, g // 2)][:, g % 2, BANK * h : BANK * (h + 1)],
+                        w_tiles[(name, g)][:, BANK * h : BANK * (h + 1)],
                         BANK * h, BANK * (h + 1),
                     )
             return z

@@ -143,16 +143,14 @@ def tile_customlstmcell_w_kernel(tc, y, h_light, c_light, h_temp, c_temp, *rest)
                         ident_f32[:],
                     )
         grouped = {}
-        for xname in ("h1", "h2", "y"):
-            grouped[xname] = keep.tile([P, 2, P, 4], BF16, name="grouped_" + xname, align_bytes=64)
-            src = x_t[xname][:].rearrange("p g u m -> p g m u")
-            if xname == "y":
-                nc.scalar.copy(out=grouped[xname][:].bitcast(F32), in_=src)
-            else:
-                nc.vector.tensor_copy(out=grouped[xname][:].bitcast(F32), in_=src)
         x_codes = {}
         x_scales = {}
-        for xname in X_NAMES:
+
+        def regroup(xname, engine_copy):
+            grouped[xname] = keep.tile([P, 2, P, 4], BF16, name="grouped_" + xname, align_bytes=64)
+            engine_copy(out=grouped[xname][:].bitcast(F32), in_=x_t[xname][:].rearrange("p g u m -> p g m u"))
+
+        def quantise(xname):
             x_codes[xname] = keep.tile([P, 2 * P], U32, name="xc_" + xname, align_bytes=64)
             x_scales[xname] = keep.tile([P, 2 * P], U8, name="xs_" + xname, align_bytes=64)
             nc.vector.quantize_mx(
@@ -160,6 +158,13 @@ def tile_customlstmcell_w_kernel(tc, y, h_light, c_light, h_temp, c_temp, *rest)
                 scales=x_scales[xname][:],
                 in_=grouped[xname][:].rearrange("p g m t -> p (g m t)"),
             )
+
+        regroup("h1", nc.vector.tensor_copy)
+        regroup("y", nc.scalar.copy)
+        quantise("h1")
+        quantise("y")
+        regroup("h2", nc.vector.tensor_copy)
+        quantise("h2")
 
         bias_bc = {}
         gate = {}

@@ -20,7 +20,7 @@ GROUPS = 4
 NAMES = ("f1", "i1", "c1", "o1", "f2", "i2", "c2", "o2")
 ORDER = ("f1", "f2", "i1", "c1", "i2", "c2", "o1", "o2")
 LAST = "o2"
-LAST_CHUNKS = ((0, 256), (256, 512), (512, 768), (768, 1024))
+LAST_CHUNKS = ((0, 256), (256, 512), (512, 768), (768, 896), (896, 1024))
 X_NAMES = ("h1", "y", "h2")
 
 FLOPS = 2 * 128 * 2048 * 8192
@@ -261,14 +261,26 @@ def tile_customlstmcell_w_kernel(tc, y, h_light, c_light, h_temp, c_temp, *rest)
             nc.scalar.activation(out=a[:], in_=a[:], func=ACT.Sigmoid)
             last[c0] = a
 
-        def last_back(c0, c1):
-            a = last[c0]
-            tt(a[:], a[:], o_first[:, c0:c1], ALU.add)
-            tt(a[:], a[:], tanh_c[:, c0:c1], ALU.mult)
-            nc.sync.dma_start(out=h_new[:, c0:c1], in_=a[:])
+        def last_sum(c0, c1):
+            tt(last[c0][:], last[c0][:], o_first[:, c0:c1], ALU.add)
 
-        for k, (c0, c1) in enumerate(LAST_CHUNKS):
-            last_front(c0, c1)
-            if k > 0:
-                last_back(*LAST_CHUNKS[k - 1])
-        last_back(*LAST_CHUNKS[-1])
+        def last_product(c0, c1):
+            tt(last[c0][:], last[c0][:], tanh_c[:, c0:c1], ALU.mult)
+            nc.sync.dma_start(out=h_new[:, c0:c1], in_=last[c0][:])
+
+        q0, q1, q2, q3, q4 = LAST_CHUNKS
+        last_front(*q0)
+        last_front(*q1)
+        last_sum(*q0)
+        last_product(*q0)
+        last_front(*q2)
+        last_sum(*q1)
+        last_front(*q3)
+        last_product(*q1)
+        last_front(*q4)
+        last_sum(*q2)
+        last_sum(*q3)
+        last_product(*q2)
+        last_sum(*q4)
+        last_product(*q3)
+        last_product(*q4)

@@ -127,7 +127,7 @@ def tile_customlstmcell_w_kernel(tc, y, h_light, c_light, h_temp, c_temp, *rest)
                 load_scales(name)
             if name == LAST:
                 for c0, c1 in LAST_CHUNKS:
-                    load_chunk(name, c0, c1, ((0, 3), (3, 4)) if c1 == H else ((0, 4),))
+                    load_chunk(name, c0, c1, ((0, 3), (3, 4)))
             else:
                 load_gate(name)
 

from contextlib import ExitStack

import concourse.mybir as mybir
from concourse.masks import make_identity

F32 = mybir.dt.float32
BF16 = mybir.dt.bfloat16
I32 = mybir.dt.int32
U32 = mybir.dt.uint32
U8 = mybir.dt.uint8
FP8X4 = mybir.dt.float8_e4m3fn_x4
ALU = mybir.AluOpType
ACT = mybir.ActivationFunctionType

P = 128
H = 1024
BANK = 512
GROUPS = 4

NAMES = ("f1", "i1", "c1", "o1", "f2", "i2", "c2", "o2")
ORDER = ("f1", "f2", "i1", "c1", "i2", "c2", "o1", "o2")
LAST = "o2"
LAST_CHUNKS = ((0, 256), (256, 512), (512, 768), (768, 896), (896, 1024))
X_NAMES = ("h1", "y", "h2")

FLOPS = 2 * 128 * 2048 * 8192
BYTES = 8 * (2048 * 1024 + 64 * 1024 + 2 * 1024) + 4 * 128 * 1024 * 2 + 2 * 128 * 1024 * 4


def tile_customlstmcell_w_kernel(tc, y, h_light, c_light, h_temp, c_temp, *rest):
    nc = tc.nc
    words = {}
    scales = {}
    biases = {}
    for i, name in enumerate(NAMES):
        words[name] = rest[3 * i]
        scales[name] = rest[3 * i + 1]
        biases[name] = rest[3 * i + 2]
    h_new = rest[24]
    c_new = rest[25]

    with ExitStack() as ctx:
        keep = ctx.enter_context(tc.tile_pool(name="keep", bufs=1))
        psum = ctx.enter_context(tc.psum_pool(name="psum", bufs=8))
        ctx.enter_context(tc.manual_schedule())

        planes = {}
        for name in ORDER:
            planes[name] = keep.tile([P, H], U8, name="plane_" + name, align_bytes=64)
        bias_rows = {}
        nc.vector.memset(planes[ORDER[0]][:].bitcast(I32), 0)
        for i in range(0, len(ORDER), 2):
            pair = keep.tile([P, H], BF16, name="bias_rows_%d" % i)
            nc.vector.memset(pair[:], 0.0)
            bias_rows[ORDER[i]] = (pair, 0)
            bias_rows[ORDER[i + 1]] = (pair, 1)
        for name in ORDER[1:]:
            nc.vector.memset(planes[name][:].bitcast(I32), 0)
        ident_f32 = keep.tile([P, P], F32, name="ident_f32")
        make_identity(nc, ident_f32[:])

        def load_bias(name):
            pair, r = bias_rows[name]
            nc.gpsimd.dma_start(out=pair[r : r + 1, :], in_=biases[name].unsqueeze(0))

        def load_scales_soft(name):
            for q in range(4):
                nc.gpsimd.dma_start(
                    out=planes[name][32 * q : 32 * q + 16, :].bitcast(F32),
                    in_=scales[name][:, 4 * q : 4 * q + 4, :].bitcast(F32),
                )

        for name in ORDER[:4]:
            load_bias(name)
        for i in range(2, len(ORDER), 2):
            load_scales_soft(ORDER[i])
            load_scales_soft(ORDER[i + 1])
            if i + 2 < len(ORDER):
                load_bias(ORDER[i + 2])
                load_bias(ORDER[i + 3])
        ident_bf16 = keep.tile([P, P], BF16, name="ident_bf16")
        nc.vector.tensor_copy(out=ident_bf16[:], in_=ident_f32[:])

        w_tiles = {}

        def load_scales(name):
            for q in range(4):
                nc.sync.dma_start(
                    out=planes[name][32 * q : 32 * q + 16, :].bitcast(I32),
                    in_=scales[name][:, 4 * q : 4 * q + 4, :].bitcast(I32),
                )

        def load_groups(name, g0, g1):
            wt = keep.tile([P, g1 - g0, H], U32, name="w_%s_%d" % (name, g0), align_bytes=64)
            nc.sync.dma_start(
                out=wt[:].bitcast(I32),
                in_=words[name][g0:g1].rearrange("g p n t -> p g (n t)").bitcast(I32),
            )
            for g in range(g0, g1):
                w_tiles[(name, g)] = wt[:, g - g0, :]

        def load_gate(name):
            for g in range(GROUPS):
                load_groups(name, g, g + 1)

        def load_chunk(name, c0, c1, cuts):
            wt = keep.tile([P, GROUPS, c1 - c0], U32, name="w_%s_%d" % (name, c0), align_bytes=64)
            for g0, g1 in cuts:
                nc.sync.dma_start(
                    out=wt[:, g0:g1, :].bitcast(I32),
                    in_=words[name][g0:g1, :, c0:c1, :].rearrange("g p n t -> p g (n t)").bitcast(I32),
                )
            w_tiles[(name, c0)] = wt

        x_in = {}
        for xname, src in (("h1", h_light), ("y", y), ("h2", h_temp)):
            x_in[xname] = keep.tile([P, H], BF16, name="x_" + xname)
            nc.sync.dma_start(out=x_in[xname][:], in_=src)
        c_in = keep.tile([P, H], BF16, name="c_in")

        load_scales(ORDER[0])
        load_gate(ORDER[0])
        nc.sync.dma_start(out=c_in[:], in_=c_light)
        for i in range(1, len(ORDER)):
            name = ORDER[i]
            if i < 2:
                load_scales(name)
            if name == LAST:
                for c0, c1 in LAST_CHUNKS:
                    load_chunk(name, c0, c1, ((0, 3), (3, 4)))
            else:
                load_gate(name)

        x_t = {}
        for xname in X_NAMES:
            x_t[xname] = psum.tile([P, 2, 2, P], F32, name="xt_" + xname, tag="bank")
            x_words = x_in[xname][:].bitcast(F32)
            for gl in range(2):
                for u in range(2):
                    nc.tensor.transpose(
                        x_t[xname][:, gl, u, :],
                        x_words[:, 256 * gl + u : 256 * (gl + 1) : 2],
                        ident_f32[:],
                    )
        grouped = {}
        x_codes = {}
        x_scales = {}

        def regroup(xname, engine_copy):
            grouped[xname] = keep.tile([P, 2, P, 4], BF16, name="grouped_" + xname, align_bytes=64)
            engine_copy(out=grouped[xname][:].bitcast(F32), in_=x_t[xname][:].rearrange("p g u m -> p g m u"))

        def quantise(xname):
            x_codes[xname] = keep.tile([P, 2 * P], U32, name="xc_" + xname, align_bytes=64)
            x_scales[xname] = keep.tile([P, 2 * P], U8, name="xs_" + xname, align_bytes=64)
            nc.vector.quantize_mx(
                out=x_codes[xname][:].bitcast(FP8X4),
                scales=x_scales[xname][:],
                in_=grouped[xname][:].rearrange("p g m t -> p (g m t)"),
            )

        regroup("h1", nc.vector.tensor_copy)
        regroup("y", nc.scalar.copy)
        quantise("h1")
        quantise("y")
        regroup("h2", nc.vector.tensor_copy)
        quantise("h2")

        bias_bc = {}
        gate = {}

        def broadcast_bias(name):
            pair, r = bias_rows[name]
            bb = psum.tile([P, H], BF16, name="bb_" + name, tag="bank")
            for h in range(2):
                nc.tensor.matmul(
                    out=bb[:, BANK * h : BANK * (h + 1)],
                    lhsT=ident_bf16[:, r : r + 1].to_broadcast([P, P]),
                    rhs=pair[:, BANK * h : BANK * (h + 1)],
                    start=True,
                    stop=True,
                )
            bias_bc[name] = keep.tile([P, H], BF16, name="bias_" + name)
            nc.scalar.copy(out=bias_bc[name][:], in_=bb[:])

        def mx_pass(out, name, g, rhs, c0, c1):
            xname = ("h1" if name[1] == "1" else "h2") if g < 2 else "y"
            gl = g % 2
            nc.tensor.matmul_mx(
                out=out,
                lhsT=x_codes[xname][:, P * gl : P * (gl + 1)].bitcast(FP8X4),
                lhsT_scale=x_scales[xname][:, P * gl : P * (gl + 1)],
                rhs=rhs.bitcast(FP8X4),
                rhs_scale=planes[name][4 * g : P, c0:c1],
                start=(g == 0),
                stop=(g == GROUPS - 1),
            )

        def gate_matmuls(name):
            z = [psum.tile([P, BANK], F32, name="z_%s_%d" % (name, h), tag="bank") for h in range(2)]
            for g in range(GROUPS):
                for h in range(2):
                    mx_pass(
                        z[h][:], name, g,
                        w_tiles[(name, g)][:, BANK * h : BANK * (h + 1)],
                        BANK * h, BANK * (h + 1),
                    )
            return z

        def halves():
            return [slice(BANK * h, BANK * (h + 1)) for h in range(2)]

        def gate_act(name, z):
            gate[name] = keep.tile([P, H], F32, name="gate_" + name)
            for h, cols in enumerate(halves()):
                nc.vector.tensor_tensor(out=gate[name][:, cols], in0=z[h][:], in1=bias_bc[name][:, cols], op=ALU.add)
            for cols in halves():
                nc.scalar.activation(
                    out=gate[name][:, cols], in_=gate[name][:, cols],
                    func=(ACT.Tanh if name[0] == "c" else ACT.Sigmoid),
                )

        def tt(out, in0, in1, op):
            nc.vector.tensor_tensor(out=out, in0=in0, in1=in1, op=op)

        z = gate_matmuls(ORDER[0])
        broadcast_bias(ORDER[0])
        broadcast_bias(ORDER[1])
        broadcast_bias(ORDER[2])
        gate_act(ORDER[0], z)
        for i in range(1, len(ORDER) - 1):
            name = ORDER[i]
            z = gate_matmuls(name)
            if i + 2 < len(ORDER):
                broadcast_bias(ORDER[i + 2])
            gate_act(name, z)
            if name == "i1":
                tt(gate["f1"][:], gate["f1"][:], gate["f2"][:], ALU.add)
                tt(gate["f2"][:], gate["f1"][:], c_in[:], ALU.mult)
            if name == "i2":
                tt(gate["i1"][:], gate["i1"][:], gate["c1"][:], ALU.mult)
                tt(gate["f2"][:], gate["i1"][:], gate["f2"][:], ALU.add)
            if name == "c2":
                for cols in halves():
                    tt(gate["i2"][:, cols], gate["i2"][:, cols], gate["c2"][:, cols], ALU.mult)
                    tt(gate["c1"][:, cols], gate["i2"][:, cols], gate["f2"][:, cols], ALU.add)
                    nc.scalar.activation(out=gate["c2"][:, cols], in_=gate["c1"][:, cols], func=ACT.Tanh)
                nc.sync.dma_start(out=c_new, in_=gate["c1"][:])

        tanh_c = gate["c2"]
        o_first = gate["o1"]
        last = {}

        def last_front(c0, c1):
            n = c1 - c0
            zl = psum.tile([P, BANK], F32, name="z_last_%d" % c0, tag="bank")
            for g in range(GROUPS):
                mx_pass(zl[:, :n], LAST, g, w_tiles[(LAST, c0)][:, g, :], c0, c1)
            a = keep.tile([P, n], F32, name="last_%d" % c0)
            tt(a[:], zl[:, :n], bias_bc[LAST][:, c0:c1], ALU.add)
            nc.scalar.activation(out=a[:], in_=a[:], func=ACT.Sigmoid)
            last[c0] = a

        def last_sum(c0, c1):
            tt(last[c0][:], last[c0][:], o_first[:, c0:c1], ALU.add)

        def last_product(c0, c1):
            tt(last[c0][:], last[c0][:], tanh_c[:, c0:c1], ALU.mult)
            nc.sync.dma_start(out=h_new[:, c0:c1], in_=last[c0][:])

        q0, q1, q2, q3, q4 = LAST_CHUNKS
        last_front(*q0)
        last_front(*q1)
        last_sum(*q0)
        last_product(*q0)
        last_front(*q2)
        last_sum(*q1)
        last_front(*q3)
        last_product(*q1)
        last_front(*q4)
        last_sum(*q2)
        last_sum(*q3)
        last_product(*q2)
        last_sum(*q4)
        last_product(*q3)
        last_product(*q4)
